import numpy as np
import ml_dtypes


def mxq(x, axis, fmt="e4m3"):
    dtype, down = {"e4m3": (ml_dtypes.float8_e4m3fn, 7), "e5m2": (ml_dtypes.float8_e5m2, 14)}[fmt]
    v = np.moveaxis(np.asarray(x, np.float32).astype(ml_dtypes.bfloat16).astype(np.float64), axis, -1)
    blocks = v.reshape(v.shape[:-1] + (-1, 32))
    amax = np.abs(blocks).max(-1, keepdims=True)
    byte = np.maximum(np.where(amax > 0, np.frexp(amax)[1] - 1 + 127, 0) - down, 1)
    scale = np.exp2(byte - 127.0)
    codes = (blocks / scale).astype(np.float32).astype(dtype).astype(np.float64)
    return np.moveaxis((codes * scale).reshape(v.shape), -1, axis)


WIDE = False


def mx_kscale(k):
    if not WIDE:
        return np.ones(k)
    levels = np.array([10, -10, 5, -5, 0])
    a = np.random.permutation(np.resize(levels, k // 512 * 4)).reshape(k // 512, 4)
    idx = np.arange(k)
    return np.exp2(a[idx // 512, idx % 128 // 32])


BF16 = ml_dtypes.bfloat16


def bf(x):
    return np.asarray(x, np.float32).astype(BF16)


def f64(x):
    return np.asarray(x).astype(np.float64)


B, F_IN, H, D, N = 1024, 768, 512, 512, 4096
C = 3.0
SQRT_C = np.sqrt(C)
MIN_NORM = 1e-15
EPS = 1e-5
TEMP = 0.07


def artanh(v):
    return 0.5 * np.log((1.0 + v) / (1.0 - v))


def expmap0(u):
    un = np.maximum(np.sqrt((u * u).sum(-1, keepdims=True)), MIN_NORM)
    return np.tanh(SQRT_C * un) * u / (SQRT_C * un)


def profile():
    d = 1.0 / np.sqrt(1.0 + np.arange(D))
    return d / np.sqrt((d * d).sum())


def setup_inputs():
    s = mx_kscale(H)
    d = profile()
    g = np.random.standard_normal((N, D)) * d
    return {"h_mlp": bf(np.random.standard_normal((B, H)) * 0.65 * s),
            "W3": bf(np.random.standard_normal((H, D)) * 0.8 / np.sqrt(H) * d / s[:, None]),
            "b3": bf(np.random.standard_normal(D) * 0.2 * d),
            "prototypes": bf(g / np.sqrt((g * g).sum(1, keepdims=True)) * 0.95 / C)}


def reference(h_mlp, W3, b3, prototypes):
    p = f64(prototypes)
    u = (mxq(f64(h_mlp), 1, "e4m3") @ mxq(f64(W3), 0, "e4m3")) + f64(b3)
    hyp = expmap0(u)
    A = (p * p).sum(-1)
    Bn = (hyp * hyp).sum(-1)
    P = mxq(hyp, 1, "e4m3") @ mxq(p, 1, "e4m3").T
    alpha = 1.0 - 2.0 * C * P + C * Bn[:, None]
    beta = 1.0 - C * A[None, :]
    denom = np.maximum(1.0 - 2.0 * C * P + (C * C) * A[None, :] * Bn[:, None], MIN_NORM)
    num_sq = alpha * alpha * A[None, :] + beta * beta * Bn[:, None] - 2.0 * alpha * beta * P
    mnorm = np.sqrt(np.maximum(num_sq, MIN_NORM)) / denom
    arg = np.minimum(SQRT_C * mnorm, 1.0 - EPS)
    dist = (2.0 / SQRT_C) * artanh(arg)
    return -dist / TEMP, hyp

@@ -1,0 +1,334 @@
+import math
+from contextlib import ExitStack
+
+import concourse.mybir as mybir
+from concourse.masks import make_identity
+
+F32 = mybir.dt.float32
+BF16 = mybir.dt.bfloat16
+U32 = mybir.dt.uint32
+U8 = mybir.dt.uint8
+FP8X4 = mybir.dt.float8_e4m3fn_x4
+ALU = mybir.AluOpType
+ACT = mybir.ActivationFunctionType
+
+P = 128
+B, H, D, N = 1024, 512, 512, 4096
+NT = B // P
+GRP = 512
+NG = N // GRP
+C = 3.0
+TEMP = 0.07
+K_OUT = 2.0 / (math.sqrt(C) * TEMP)
+ARG_MAX = 1.0 - 1e-5
+LOGIT_MIN = -(1.0 / (math.sqrt(C) * TEMP)) * math.log((1.0 + ARG_MAX) / (1.0 - ARG_MAX))
+EDGE = 1e-6
+
+FLOPS = 2 * B * H * D + 2 * B * N * D
+
+BLOCKS = (4, 4)
+T_BUFS = 4
+Y_BUFS = 10
+MANUAL = False
+A_ENG = "SSSSSSVV"
+
+
+def tile_hyperbolicuniform_pa_kernel(tc, h_mlp, W3, b3, prototypes, out_0, out_1):
+    nc = tc.nc
+    with ExitStack() as ctx:
+        if MANUAL:
+            ctx.enter_context(tc.manual_schedule())
+        keep = ctx.enter_context(tc.tile_pool(name="keep", bufs=1))
+        ring = ctx.enter_context(tc.tile_pool(name="ring", bufs=1))
+        psum = ctx.enter_context(tc.psum_pool(name="psum", bufs=1))
+
+        h_v = h_mlp.rearrange("(p t) k -> p t k", t=NT)
+        w_v = W3.rearrange("(u q e) c -> q u (e c)", u=2, e=2)
+        p_v = prototypes.rearrange("(r p) d -> p r d", p=P)
+        lg_v = out_0.rearrange("(p t) j -> p t j", t=NT)
+        hy_v = out_1.rearrange("(p t) d -> p t d", t=NT)
+
+        ident = keep.tile([P, P], F32, name="ident")
+        b_bc = keep.tile([P, D], BF16, name="b_bc")
+        w_raw = keep.tile([P, 2, 2 * D], BF16, name="w_raw")
+        w_grp = keep.tile([P, D, 4], BF16, name="w_grp", align_bytes=64)
+        w_codes = keep.tile([P, D], U32, name="w_codes", align_bytes=64)
+        w_scales = keep.tile([P, D], U8, name="w_scales", align_bytes=64)
+        h_codes = keep.tile([P, B], U32, name="h_codes", align_bytes=64)
+        h_scales = keep.tile([P, B], U8, name="h_scales", align_bytes=64)
+        y_codes = keep.tile([P, B], U32, name="y_codes", align_bytes=64)
+        y_scales = keep.tile([P, B], U8, name="y_scales", align_bytes=64)
+        p_codes = keep.tile([P, N], U32, name="p_codes", align_bytes=64)
+        p_scales = keep.tile([P, N], U8, name="p_scales", align_bytes=64)
+        q_sb = keep.tile([P, N], F32, name="q_sb")
+        junk_s = keep.tile([P, D], BF16, name="junk_s")
+        junk_v = keep.tile([P, D], F32, name="junk_v")
+        warm = keep.tile([P, 1], F32, name="warm")
+        warm2 = keep.tile([P, 1], F32, name="warm2")
+
+        def stat(name, w=NT):
+            return keep.tile([P, w], F32, name=name)
+
+        ss, cs, xx, th, rx, sc = stat("ss"), stat("cs"), stat("xx"), stat("th"), stat("rx"), stat("sc")
+        s2, bn, ee, be, rr, nr, omr = stat("s2"), stat("bn"), stat("ee"), stat("be"), stat("rr"), stat("nr"), stat("omr")
+        a_g = [stat("a_g%d" % g, 4) for g in range(NG)]
+        q_g = [stat("q_g%d" % g, 4) for g in range(NG)]
+
+        nc.sync.dma_start(out=w_raw, in_=w_v)
+        h_sb = ring.tile([P, NT, H], BF16, name="h_sb", tag="y", bufs=Y_BUFS, align_bytes=64)
+        nc.sync.dma_start(out=h_sb[:, 0:4, :], in_=h_v[:, 0:4, :])
+        nc.sync.dma_start(out=h_sb[:, 4:8, :], in_=h_v[:, 4:8, :])
+        p_sb = []
+        for k in range(4):
+            pt = ring.tile([P, 8, D], BF16, name="p_sb%d" % k, tag="p_sb", bufs=4)
+            nc.sync.dma_start(out=pt, in_=p_v[:, 8 * k : 8 * k + 8, :])
+            p_sb.append(pt)
+        nc.scalar.dma_start(out=b_bc, in_=b3.partition_broadcast(P))
+        make_identity(nc, ident)
+        nc.vector.memset(warm, 1.0)
+        nc.scalar.activation(out=warm2, in_=warm, func=ACT.Sqrt)
+
+        def copy_out(eng, out, in_):
+            if eng == "V":
+                nc.vector.tensor_copy(out=out, in_=in_)
+            else:
+                nc.scalar.copy(out=out, in_=in_)
+
+        def w3_prep():
+            nc.vector.tensor_copy(
+                out=w_grp.rearrange("p (c i) t -> p c t i", i=4),
+                in_=w_raw.rearrange("p u (e c i) -> p c (u e) i", e=2, i=4),
+            )
+            nc.vector.quantize_mx(out=w_codes.bitcast(FP8X4), scales=w_scales, in_=w_grp.rearrange("p c t -> p (c t)"))
+
+        g_h = ring.tile([P, B, 2], F32, name="g_h", tag="y", bufs=Y_BUFS, align_bytes=64)
+
+        def h_transpose(tp, eng):
+            ps = psum.tile([P, 2, 2, P], F32, name="tr_h", tag="tr", bufs=2)
+            for a in range(2):
+                words = h_sb[:, 2 * tp + a, :].bitcast(F32)
+                for u in range(2):
+                    nc.tensor.transpose(ps[:, a, u, :], words[:, P * u : P * u + P], ident)
+            copy_out(
+                eng,
+                g_h[:, 2 * P * tp : 2 * P * tp + 2 * P, :].rearrange("p (a i) u -> p a i u", a=2),
+                ps.rearrange("p a u i -> p a i u"),
+            )
+
+        def h_quant(hf):
+            cols = slice(512 * hf, 512 * hf + 512)
+            nc.vector.quantize_mx(
+                out=h_codes[:, cols].bitcast(FP8X4),
+                scales=h_scales[:, cols],
+                in_=g_h[:, cols, :].rearrange("p i u -> p (i u)").bitcast(BF16),
+            )
+
+        hy = [ring.tile([P, 4, D], F32, name="hy%d" % hf, tag="y", bufs=Y_BUFS, align_bytes=64) for hf in range(2)]
+
+        def u_tile(t):
+            rows = slice(P * t, P * t + P)
+            u_ps = psum.tile([P, D], F32, name="u_ps", tag="pp", bufs=4)
+            nc.tensor.matmul_mx(
+                out=u_ps,
+                lhsT=h_codes[:, rows].bitcast(FP8X4),
+                lhsT_scale=h_scales[:, rows],
+                rhs=w_codes.bitcast(FP8X4),
+                rhs_scale=w_scales,
+                start=True,
+                stop=True,
+            )
+            ub = hy[t // 4][:, t % 4, :]
+            nc.vector.tensor_tensor(out=ub, in0=u_ps, in1=b_bc, op=ALU.add)
+            nc.scalar.activation(out=junk_s, in_=ub, func=ACT.Square, accum_out=ss[:, t : t + 1])
+
+        def row_stats():
+            nc.vector.tensor_scalar(out=cs, in0=ss, scalar1=C, scalar2=C * 1e-30, op0=ALU.mult, op1=ALU.max)
+            nc.scalar.activation(out=xx, in_=cs, func=ACT.Sqrt)
+            nc.scalar.activation(out=th, in_=xx, func=ACT.Tanh)
+            nc.vector.reciprocal(out=rx, in_=xx)
+            nc.vector.tensor_tensor(out=sc, in0=th, in1=rx, op=ALU.mult)
+
+        def row_stats2():
+            nc.vector.tensor_tensor(out=s2, in0=sc, in1=sc, op=ALU.mult)
+            nc.vector.tensor_tensor(out=bn, in0=s2, in1=ss, op=ALU.mult)
+            nc.vector.tensor_scalar(out=ee, in0=bn, scalar1=1.0 / C, scalar2=0.5, op0=ALU.add, op1=ALU.mult)
+            nc.vector.tensor_scalar(out=be, in0=bn, scalar1=-C, scalar2=1.0, op0=ALU.mult, op1=ALU.add)
+            nc.vector.tensor_scalar(out=be, in0=be, scalar1=EDGE, scalar2=None, op0=ALU.max)
+            nc.vector.reciprocal(out=rr, in_=be)
+            nc.vector.tensor_scalar(out=nr, in0=rr, scalar1=-1.0, scalar2=None, op0=ALU.mult)
+            nc.vector.tensor_scalar(out=omr, in0=rr, scalar1=-1.0, scalar2=1.0, op0=ALU.mult, op1=ALU.add)
+
+        g_y = ring.tile([P, B, 4], BF16, name="g_y", tag="y", bufs=Y_BUFS, align_bytes=64)
+
+        def hyp_scale(t):
+            ub = hy[t // 4][:, t % 4, :]
+            nc.vector.tensor_scalar(out=ub, in0=ub, scalar1=sc[:, t : t + 1], scalar2=None, op0=ALU.mult)
+
+        def hyp_transpose(t, eng):
+            src = hy[t // 4][:, t % 4, :].rearrange("p (u m e) -> p u e m", u=2, e=2)
+            ps = psum.tile([P, 4, P], F32, name="tr_y", tag="tr", bufs=2)
+            for u in range(2):
+                for e in range(2):
+                    nc.tensor.transpose(ps[:, 2 * u + e, :], src[:, u, e, :], ident)
+            copy_out(eng, g_y[:, P * t : P * t + P, :], ps.rearrange("p t i -> p i t"))
+
+        def hyp_quant(hf):
+            cols = slice(512 * hf, 512 * hf + 512)
+            nc.vector.quantize_mx(
+                out=y_codes[:, cols].bitcast(FP8X4),
+                scales=y_scales[:, cols],
+                in_=g_y[:, cols, :].rearrange("p i t -> p (i t)"),
+            )
+
+        g_p = {}
+
+        def p_transpose(g, hb, eng):
+            if hb == 0:
+                g_p[g] = ring.tile([P, GRP, 2], F32, name="g_p", tag="g_p", bufs=2, align_bytes=64)
+            ps = psum.tile([P, 2, 2, P], F32, name="tr_p", tag="tr", bufs=2)
+            for a in range(2):
+                r = 4 * g + 2 * hb + a
+                words = p_sb[r // 8][:, r % 8, :].bitcast(F32)
+                for u in range(2):
+                    nc.tensor.transpose(ps[:, a, u, :], words[:, P * u : P * u + P], ident)
+            copy_out(
+                eng,
+                g_p[g][:, 2 * P * hb : 2 * P * hb + 2 * P, :].rearrange("p (a j) u -> p a j u", a=2),
+                ps.rearrange("p a u j -> p a j u"),
+            )
+
+        def p_quant(g):
+            cols = slice(GRP * g, GRP * g + GRP)
+            nc.vector.quantize_mx(
+                out=p_codes[:, cols].bitcast(FP8X4),
+                scales=p_scales[:, cols],
+                in_=g_p[g].rearrange("p j u -> p (j u)").bitcast(BF16),
+            )
+
+        def p_norm(g, a):
+            r = 4 * g + a
+            rows = p_sb[r // 8][:, r % 8, :]
+            if A_ENG[g] == "S":
+                nc.scalar.activation(out=junk_s, in_=rows, func=ACT.Square, accum_out=a_g[g][:, a : a + 1])
+            else:
+                nc.vector.scalar_tensor_tensor(
+                    out=junk_v, in0=rows, scalar=1.0, in1=rows, op0=ALU.mult, op1=ALU.mult, accum_out=a_g[g][:, a : a + 1]
+                )
+
+        def p_factor(g, eng):
+            nc.vector.tensor_scalar(out=q_g[g], in0=a_g[g], scalar1=(1.0 - EDGE) / C, scalar2=0.5, op0=ALU.min, op1=ALU.mult)
+            nc.vector.tensor_scalar(out=q_g[g], in0=q_g[g], scalar1=-0.5 / C, scalar2=None, op0=ALU.add)
+            nc.vector.reciprocal(out=q_g[g], in_=q_g[g])
+            qb = psum.tile([P, GRP], F32, name="qb", tag="qb", bufs=2)
+            for a in range(4):
+                nc.tensor.matmul(
+                    out=qb[:, P * a : P * a + P],
+                    lhsT=q_g[g][:, a : a + 1].to_broadcast([P, P]),
+                    rhs=ident,
+                    start=True,
+                    stop=True,
+                )
+            copy_out(eng, q_sb[:, GRP * g : GRP * g + GRP], qb)
+
+        def p_group(g, e0="V", e1="S", e2="V"):
+            p_transpose(g, 0, e0)
+            p_transpose(g, 1, e1)
+            for a in range(4):
+                p_norm(g, a)
+            p_quant(g)
+            p_factor(g, e2)
+
+        t_tiles, y_tiles = {}, {}
+
+        def products(b, g0, ng, t):
+            rows = slice(P * t, P * t + P)
+            tt = ring.tile([P, ng * GRP], F32, name="tt", tag="tt", bufs=T_BUFS)
+            t_tiles[(b, t)] = tt
+            for l in range(ng):
+                cols = slice(GRP * (g0 + l), GRP * (g0 + l) + GRP)
+                pp = psum.tile([P, GRP], F32, name="pp", tag="pp", bufs=4)
+                nc.tensor.matmul_mx(
+                    out=pp,
+                    lhsT=y_codes[:, rows].bitcast(FP8X4),
+                    lhsT_scale=y_scales[:, rows],
+                    rhs=p_codes[:, cols].bitcast(FP8X4),
+                    rhs_scale=p_scales[:, cols],
+                    start=True,
+                    stop=True,
+                )
+                nc.vector.scalar_tensor_tensor(
+                    out=tt[:, GRP * l : GRP * l + GRP],
+                    in0=pp,
+                    scalar=ee[:, t : t + 1],
+                    in1=q_sb[:, cols],
+                    op0=ALU.subtract,
+                    op1=ALU.mult,
+                )
+
+        gate_rr = {0: rr}
+        gate_ln = {}
+
+        def gate(name, probe):
+            z = keep.tile([P, 1], F32, name=name)
+            nc.gpsimd.tensor_scalar(out=z, in0=probe, scalar1=0.0, scalar2=0.0, op0=ALU.min, op1=ALU.max)
+            return z
+
+        def roots(b, ng, t):
+            rr = gate_rr[b]
+            tt = t_tiles[(b, t)]
+            yy = ring.tile([P, ng * GRP], F32, name="yy", tag="y", bufs=Y_BUFS, align_bytes=64)
+            y_tiles[(b, t)] = yy
+            nc.scalar.activation(out=yy, in_=tt, func=ACT.Sqrt, scale=rr[:, t : t + 1], bias=nr[:, t : t + 1])
+            nc.scalar.activation(out=tt, in_=tt, func=ACT.Sqrt, scale=rr[:, t : t + 1], bias=omr[:, t : t + 1])
+
+        def add_roots(b, t):
+            yy = y_tiles[(b, t)]
+            nc.vector.scalar_tensor_tensor(out=yy, in0=yy, scalar=0.0, in1=t_tiles[(b, t)], op0=ALU.max, op1=ALU.add)
+
+        def log_(b, t):
+            yy = y_tiles[(b, t)]
+            nc.scalar.activation(out=yy, in_=yy, func=ACT.Ln, bias=gate_ln[b])
+
+        def finish(b, g0, ng, t):
+            yy = y_tiles[(b, t)]
+            nc.vector.tensor_scalar(out=yy, in0=yy, scalar1=-K_OUT, scalar2=LOGIT_MIN, op0=ALU.mult, op1=ALU.max)
+            nc.sync.dma_start(out=lg_v[:, t, GRP * g0 : GRP * (g0 + ng)], in_=yy)
+
+        w3_prep()
+        h_transpose(0, "V")
+        h_transpose(1, "S")
+        h_quant(0)
+        h_transpose(2, "V")
+        h_transpose(3, "S")
+        h_quant(1)
+        for t in range(NT):
+            u_tile(t)
+        row_stats()
+        for t in range(NT):
+            hyp_scale(t)
+            hyp_transpose(t, "V" if t % 2 else "S")
+            if t % 4 == 3:
+                nc.sync.dma_start(out=hy_v[:, t - 3 : t + 1, :], in_=hy[t // 4])
+                hyp_quant(t // 4)
+        row_stats2()
+        for g in range(BLOCKS[0]):
+            p_group(g)
+
+        g0 = 0
+        for b, ng in enumerate(BLOCKS):
+            for t in range(NT):
+                products(b, g0, ng, t)
+                roots(b, ng, t)
+                add_roots(b, t)
+            gate_ln[b] = gate("gate_ln%d" % b, t_tiles[(b, NT - 1)][:, 0:1])
+            for t in range(NT):
+                log_(b, t)
+                if t == NT - 1 and b + 1 < len(BLOCKS):
+                    z = gate("gate_z%d" % b, y_tiles[(b, t)][:, 0:1])
+                    gate_rr[b + 1] = stat("rr%d" % (b + 1))
+                    nc.vector.tensor_scalar(out=gate_rr[b + 1], in0=rr, scalar1=z, scalar2=None, op0=ALU.add)
+                finish(b, g0, ng, t)
+            if b + 1 < len(BLOCKS):
+                for g in range(g0 + ng, g0 + ng + BLOCKS[b + 1]):
+                    p_group(g, "V", "V", "V")
+            g0 += ng

@@ -30,7 +30,19 @@ BLOCKS = (4, 4)
 T_BUFS = 4
 Y_BUFS = 10
 MANUAL = False
+PP_BUFS = 5
+QB_BUFS = 1
+LOADS = ("w", "h0", "h1", "p0", "p1", "p2", "p3")
+H_COPY = "VSVS"
+Y_COPY = "SVSVSVSV"
+P_COPY = ("VS", "VS", "VS", "VS", "VV", "VV", "VV", "VV")
+Q_COPY = "VVVVVVVV"
+SCALE_ENG = "VVVVVVVV"
+LAST_SPLIT = 1
 A_ENG = "SSSSSSVV"
+G_FIN = "GGGGGGGG"
+G_CLAMP = True
+Y_MAX = math.sqrt((1.0 + ARG_MAX) / (1.0 - ARG_MAX))
 
 
 def tile_hyperbolicuniform_pa_kernel(tc, h_mlp, W3, b3, prototypes, out_0, out_1):
@@ -74,15 +86,17 @@ def tile_hyperbolicuniform_pa_kernel(tc, h_mlp, W3, b3, prototypes, out_0, out_1
         a_g = [stat("a_g%d" % g, 4) for g in range(NG)]
         q_g = [stat("q_g%d" % g, 4) for g in range(NG)]
 
-        nc.sync.dma_start(out=w_raw, in_=w_v)
         h_sb = ring.tile([P, NT, H], BF16, name="h_sb", tag="y", bufs=Y_BUFS, align_bytes=64)
-        nc.sync.dma_start(out=h_sb[:, 0:4, :], in_=h_v[:, 0:4, :])
-        nc.sync.dma_start(out=h_sb[:, 4:8, :], in_=h_v[:, 4:8, :])
-        p_sb = []
-        for k in range(4):
-            pt = ring.tile([P, 8, D], BF16, name="p_sb%d" % k, tag="p_sb", bufs=4)
-            nc.sync.dma_start(out=pt, in_=p_v[:, 8 * k : 8 * k + 8, :])
-            p_sb.append(pt)
+        p_sb = [ring.tile([P, 8, D], BF16, name="p_sb%d" % k, tag="p_sb", bufs=4) for k in range(4)]
+        for what in LOADS:
+            if what == "w":
+                nc.sync.dma_start(out=w_raw, in_=w_v)
+            elif what[0] == "h":
+                k = int(what[1])
+                nc.sync.dma_start(out=h_sb[:, 4 * k : 4 * k + 4, :], in_=h_v[:, 4 * k : 4 * k + 4, :])
+            else:
+                k = int(what[1])
+                nc.sync.dma_start(out=p_sb[k], in_=p_v[:, 8 * k : 8 * k + 8, :])
         nc.scalar.dma_start(out=b_bc, in_=b3.partition_broadcast(P))
         make_identity(nc, ident)
         nc.vector.memset(warm, 1.0)
@@ -104,7 +118,7 @@ def tile_hyperbolicuniform_pa_kernel(tc, h_mlp, W3, b3, prototypes, out_0, out_1
         g_h = ring.tile([P, B, 2], F32, name="g_h", tag="y", bufs=Y_BUFS, align_bytes=64)
 
         def h_transpose(tp, eng):
-            ps = psum.tile([P, 2, 2, P], F32, name="tr_h", tag="tr", bufs=2)
+            ps = psum.tile([P, 2, 2, P], F32, name="tr_h", tag="pp", bufs=PP_BUFS)
             for a in range(2):
                 words = h_sb[:, 2 * tp + a, :].bitcast(F32)
                 for u in range(2):
@@ -127,7 +141,7 @@ def tile_hyperbolicuniform_pa_kernel(tc, h_mlp, W3, b3, prototypes, out_0, out_1
 
         def u_tile(t):
             rows = slice(P * t, P * t + P)
-            u_ps = psum.tile([P, D], F32, name="u_ps", tag="pp", bufs=4)
+            u_ps = psum.tile([P, D], F32, name="u_ps", tag="pp", bufs=PP_BUFS)
             nc.tensor.matmul_mx(
                 out=u_ps,
                 lhsT=h_codes[:, rows].bitcast(FP8X4),
@@ -162,11 +176,14 @@ def tile_hyperbolicuniform_pa_kernel(tc, h_mlp, W3, b3, prototypes, out_0, out_1
 
         def hyp_scale(t):
             ub = hy[t // 4][:, t % 4, :]
-            nc.vector.tensor_scalar(out=ub, in0=ub, scalar1=sc[:, t : t + 1], scalar2=None, op0=ALU.mult)
+            if SCALE_ENG[t] == "V":
+                nc.vector.tensor_scalar(out=ub, in0=ub, scalar1=sc[:, t : t + 1], scalar2=None, op0=ALU.mult)
+            else:
+                nc.scalar.activation(out=ub, in_=ub, func=ACT.Copy, scale=sc[:, t : t + 1])
 
         def hyp_transpose(t, eng):
             src = hy[t // 4][:, t % 4, :].rearrange("p (u m e) -> p u e m", u=2, e=2)
-            ps = psum.tile([P, 4, P], F32, name="tr_y", tag="tr", bufs=2)
+            ps = psum.tile([P, 4, P], F32, name="tr_y", tag="pp", bufs=PP_BUFS)
             for u in range(2):
                 for e in range(2):
                     nc.tensor.transpose(ps[:, 2 * u + e, :], src[:, u, e, :], ident)
@@ -219,7 +236,7 @@ def tile_hyperbolicuniform_pa_kernel(tc, h_mlp, W3, b3, prototypes, out_0, out_1
             nc.vector.tensor_scalar(out=q_g[g], in0=a_g[g], scalar1=(1.0 - EDGE) / C, scalar2=0.5, op0=ALU.min, op1=ALU.mult)
             nc.vector.tensor_scalar(out=q_g[g], in0=q_g[g], scalar1=-0.5 / C, scalar2=None, op0=ALU.add)
             nc.vector.reciprocal(out=q_g[g], in_=q_g[g])
-            qb = psum.tile([P, GRP], F32, name="qb", tag="qb", bufs=2)
+            qb = psum.tile([P, GRP], F32, name="qb", tag="qb", bufs=QB_BUFS)
             for a in range(4):
                 nc.tensor.matmul(
                     out=qb[:, P * a : P * a + P],
@@ -246,7 +263,7 @@ def tile_hyperbolicuniform_pa_kernel(tc, h_mlp, W3, b3, prototypes, out_0, out_1
             t_tiles[(b, t)] = tt
             for l in range(ng):
                 cols = slice(GRP * (g0 + l), GRP * (g0 + l) + GRP)
-                pp = psum.tile([P, GRP], F32, name="pp", tag="pp", bufs=4)
+                pp = psum.tile([P, GRP], F32, name="pp", tag="pp", bufs=PP_BUFS)
                 nc.tensor.matmul_mx(
                     out=pp,
                     lhsT=y_codes[:, rows].bitcast(FP8X4),
@@ -284,35 +301,48 @@ def tile_hyperbolicuniform_pa_kernel(tc, h_mlp, W3, b3, prototypes, out_0, out_1
         def add_roots(b, t):
             yy = y_tiles[(b, t)]
             nc.vector.scalar_tensor_tensor(out=yy, in0=yy, scalar=0.0, in1=t_tiles[(b, t)], op0=ALU.max, op1=ALU.add)
+            if G_CLAMP:
+                nc.gpsimd.tensor_scalar(out=yy, in0=yy, scalar1=Y_MAX, scalar2=1.0, op0=ALU.min, op1=ALU.max)
 
-        def log_(b, t):
+        def log_(b, t, part=None):
             yy = y_tiles[(b, t)]
+            if part is not None:
+                yy = yy[:, part[0] : part[1]]
             nc.scalar.activation(out=yy, in_=yy, func=ACT.Ln, bias=gate_ln[b])
 
-        def finish(b, g0, ng, t):
+        def finish(b, g0, ng, t, part=None):
             yy = y_tiles[(b, t)]
-            nc.vector.tensor_scalar(out=yy, in0=yy, scalar1=-K_OUT, scalar2=LOGIT_MIN, op0=ALU.mult, op1=ALU.max)
+            if part is not None:
+                yy = yy[:, part[0] : part[1]]
+                nc.vector.tensor_scalar(out=yy, in0=yy, scalar1=-K_OUT, scalar2=LOGIT_MIN, op0=ALU.mult, op1=ALU.max)
+                nc.sync.dma_start(out=lg_v[:, t, GRP * g0 + part[0] : GRP * g0 + part[1]], in_=yy)
+                return
+            k_out = -K_OUT
+            if G_CLAMP and G_FIN[t] == "G":
+                nc.gpsimd.tensor_scalar(out=yy, in0=yy, scalar1=k_out, scalar2=0.0, op0=ALU.mult, op1=ALU.add)
+            else:
+                nc.vector.tensor_scalar(out=yy, in0=yy, scalar1=k_out, scalar2=LOGIT_MIN, op0=ALU.mult, op1=ALU.max)
             nc.sync.dma_start(out=lg_v[:, t, GRP * g0 : GRP * (g0 + ng)], in_=yy)
 
         w3_prep()
-        h_transpose(0, "V")
-        h_transpose(1, "S")
+        h_transpose(0, H_COPY[0])
+        h_transpose(1, H_COPY[1])
         h_quant(0)
-        h_transpose(2, "V")
-        h_transpose(3, "S")
+        h_transpose(2, H_COPY[2])
+        h_transpose(3, H_COPY[3])
         h_quant(1)
         for t in range(NT):
             u_tile(t)
         row_stats()
         for t in range(NT):
             hyp_scale(t)
-            hyp_transpose(t, "V" if t % 2 else "S")
+            hyp_transpose(t, Y_COPY[t])
             if t % 4 == 3:
                 nc.sync.dma_start(out=hy_v[:, t - 3 : t + 1, :], in_=hy[t // 4])
                 hyp_quant(t // 4)
         row_stats2()
         for g in range(BLOCKS[0]):
-            p_group(g)
+            p_group(g, P_COPY[g][0], P_COPY[g][1], Q_COPY[g])
 
         g0 = 0
         for b, ng in enumerate(BLOCKS):
@@ -322,13 +352,19 @@ def tile_hyperbolicuniform_pa_kernel(tc, h_mlp, W3, b3, prototypes, out_0, out_1
                 add_roots(b, t)
             gate_ln[b] = gate("gate_ln%d" % b, t_tiles[(b, NT - 1)][:, 0:1])
             for t in range(NT):
+                if t == NT - 1 and b + 1 == len(BLOCKS) and LAST_SPLIT > 1:
+                    w = ng * GRP // LAST_SPLIT
+                    for k in range(LAST_SPLIT):
+                        log_(b, t, (w * k, w * k + w))
+                        finish(b, g0, ng, t, (w * k, w * k + w))
+                    continue
                 log_(b, t)
                 if t == NT - 1 and b + 1 < len(BLOCKS):
                     z = gate("gate_z%d" % b, y_tiles[(b, t)][:, 0:1])
                     gate_rr[b + 1] = stat("rr%d" % (b + 1))
-                    nc.vector.tensor_scalar(out=gate_rr[b + 1], in0=rr, scalar1=z, scalar2=None, op0=ALU.add)
+                    nc.gpsimd.tensor_scalar(out=gate_rr[b + 1], in0=rr, scalar1=z, scalar2=0.0, op0=ALU.add, op1=ALU.add)
                 finish(b, g0, ng, t)
             if b + 1 < len(BLOCKS):
                 for g in range(g0 + ng, g0 + ng + BLOCKS[b + 1]):
-                    p_group(g, "V", "V", "V")
+                    p_group(g, P_COPY[g][0], P_COPY[g][1], Q_COPY[g])
             g0 += ng

@@ -26,22 +26,24 @@ EDGE = 1e-6
 
 FLOPS = 2 * B * H * D + 2 * B * N * D
 
-BLOCKS = (4, 4)
-T_BUFS = 4
+BLOCKS = (3, 3, 2)
+T_BUFS = 5
 Y_BUFS = 10
 MANUAL = False
-PP_BUFS = 5
+AHEAD = 2
+PP_BUFS = 4
 QB_BUFS = 1
+GP_BUFS = 3
 LOADS = ("w", "h0", "h1", "p0", "p1", "p2", "p3")
 H_COPY = "VSVS"
 Y_COPY = "SVSVSVSV"
 P_COPY = ("VS", "VS", "VS", "VS", "VV", "VV", "VV", "VV")
 Q_COPY = "VVVVVVVV"
 SCALE_ENG = "VVVVVVVV"
-LAST_SPLIT = 1
-A_ENG = "SSSSSSVV"
+LAST_SPLIT = 4
+A_ENG = "SSSSPPPP"
 G_FIN = "GGGGGGGG"
-G_CLAMP = True
+G_CLAMP = False
 Y_MAX = math.sqrt((1.0 + ARG_MAX) / (1.0 - ARG_MAX))
 
 
@@ -62,8 +64,8 @@ def tile_hyperbolicuniform_pa_kernel(tc, h_mlp, W3, b3, prototypes, out_0, out_1
 
         ident = keep.tile([P, P], F32, name="ident")
         b_bc = keep.tile([P, D], BF16, name="b_bc")
-        w_raw = keep.tile([P, 2, 2 * D], BF16, name="w_raw")
-        w_grp = keep.tile([P, D, 4], BF16, name="w_grp", align_bytes=64)
+        w_raw = ring.tile([P, 2, 2 * D], BF16, name="w_raw", tag="tt", bufs=T_BUFS, align_bytes=64)
+        w_grp = ring.tile([P, D, 4], BF16, name="w_grp", tag="tt", bufs=T_BUFS, align_bytes=64)
         w_codes = keep.tile([P, D], U32, name="w_codes", align_bytes=64)
         w_scales = keep.tile([P, D], U8, name="w_scales", align_bytes=64)
         h_codes = keep.tile([P, B], U32, name="h_codes", align_bytes=64)
@@ -74,7 +76,8 @@ def tile_hyperbolicuniform_pa_kernel(tc, h_mlp, W3, b3, prototypes, out_0, out_1
         p_scales = keep.tile([P, N], U8, name="p_scales", align_bytes=64)
         q_sb = keep.tile([P, N], F32, name="q_sb")
         junk_s = keep.tile([P, D], BF16, name="junk_s")
-        junk_v = keep.tile([P, D], F32, name="junk_v")
+        junk_v = keep.tile([P, D], F32, name="junk_v") if "V" in A_ENG else None
+        junk_d = keep.tile([P, P], F32, name="junk_d")
         warm = keep.tile([P, 1], F32, name="warm")
         warm2 = keep.tile([P, 1], F32, name="warm2")
 
@@ -201,7 +204,7 @@ def tile_hyperbolicuniform_pa_kernel(tc, h_mlp, W3, b3, prototypes, out_0, out_1
 
         def p_transpose(g, hb, eng):
             if hb == 0:
-                g_p[g] = ring.tile([P, GRP, 2], F32, name="g_p", tag="g_p", bufs=2, align_bytes=64)
+                g_p[g] = ring.tile([P, GRP, 2], F32, name="g_p", tag="g_p", bufs=GP_BUFS, align_bytes=64)
             ps = psum.tile([P, 2, 2, P], F32, name="tr_p", tag="tr", bufs=2)
             for a in range(2):
                 r = 4 * g + 2 * hb + a
@@ -232,26 +235,35 @@ def tile_hyperbolicuniform_pa_kernel(tc, h_mlp, W3, b3, prototypes, out_0, out_1
                     out=junk_v, in0=rows, scalar=1.0, in1=rows, op0=ALU.mult, op1=ALU.mult, accum_out=a_g[g][:, a : a + 1]
                 )
 
+        def p_norm_pe(g):
+            ga = psum.tile([P, 4, P], F32, name="ga", tag="ga", bufs=1)
+            vals = g_p[g].rearrange("p j u -> p (j u)").bitcast(BF16).rearrange("p (j t) -> p j t", t=4)
+            for a in range(4):
+                for t in range(4):
+                    cols = vals[:, P * a : P * a + P, t]
+                    nc.tensor.matmul(out=ga[:, a, :], lhsT=cols, rhs=cols, start=(t == 0), stop=(t == 3))
+            for a in range(4):
+                nc.vector.scalar_tensor_tensor(
+                    out=junk_d, in0=ga[:, a, :], scalar=1.0, in1=ident, op0=ALU.mult, op1=ALU.mult, accum_out=a_g[g][:, a : a + 1]
+                )
+
         def p_factor(g, eng):
             nc.vector.tensor_scalar(out=q_g[g], in0=a_g[g], scalar1=(1.0 - EDGE) / C, scalar2=0.5, op0=ALU.min, op1=ALU.mult)
             nc.vector.tensor_scalar(out=q_g[g], in0=q_g[g], scalar1=-0.5 / C, scalar2=None, op0=ALU.add)
             nc.vector.reciprocal(out=q_g[g], in_=q_g[g])
             qb = psum.tile([P, GRP], F32, name="qb", tag="qb", bufs=QB_BUFS)
             for a in range(4):
-                nc.tensor.matmul(
-                    out=qb[:, P * a : P * a + P],
-                    lhsT=q_g[g][:, a : a + 1].to_broadcast([P, P]),
-                    rhs=ident,
-                    start=True,
-                    stop=True,
-                )
+                nc.tensor.transpose(qb[:, P * a : P * a + P], q_g[g][:, a : a + 1].to_broadcast([P, P]), ident)
             copy_out(eng, q_sb[:, GRP * g : GRP * g + GRP], qb)
 
         def p_group(g, e0="V", e1="S", e2="V"):
             p_transpose(g, 0, e0)
             p_transpose(g, 1, e1)
-            for a in range(4):
-                p_norm(g, a)
+            if A_ENG[g] == "P":
+                p_norm_pe(g)
+            else:
+                for a in range(4):
+                    p_norm(g, a)
             p_quant(g)
             p_factor(g, e2)
 
@@ -259,7 +271,7 @@ def tile_hyperbolicuniform_pa_kernel(tc, h_mlp, W3, b3, prototypes, out_0, out_1
 
         def products(b, g0, ng, t):
             rows = slice(P * t, P * t + P)
-            tt = ring.tile([P, ng * GRP], F32, name="tt", tag="tt", bufs=T_BUFS)
+            tt = ring.tile([P, ng * GRP], F32, name="tt", tag="tt", bufs=T_BUFS, align_bytes=64)
             t_tiles[(b, t)] = tt
             for l in range(ng):
                 cols = slice(GRP * (g0 + l), GRP * (g0 + l) + GRP)
@@ -346,9 +358,12 @@ def tile_hyperbolicuniform_pa_kernel(tc, h_mlp, W3, b3, prototypes, out_0, out_1
 
         g0 = 0
         for b, ng in enumerate(BLOCKS):
-            for t in range(NT):
+            for t in range(min(AHEAD, NT)):
                 products(b, g0, ng, t)
+            for t in range(NT):
                 roots(b, ng, t)
+                if t + AHEAD < NT:
+                    products(b, g0, ng, t + AHEAD)
                 add_roots(b, t)
             gate_ln[b] = gate("gate_ln%d" % b, t_tiles[(b, NT - 1)][:, 0:1])
             for t in range(NT):

@@ -26,24 +26,30 @@ EDGE = 1e-6
 
 FLOPS = 2 * B * H * D + 2 * B * N * D
 
-BLOCKS = (3, 3, 2)
-T_BUFS = 5
-Y_BUFS = 10
+BLOCKS = (8,)
+SUB = 4
+LN_W = 1024
+PS_BUFS = 4
+PREP_T = 6
+T_BUFS = 3
+Y_BUFS = 8
 MANUAL = False
+X_TOP = 16.0
+DOUBLINGS = 8
+TERMS = 7
+INV_FACT = (1.0, 1.0, 1.0 / 2.0, 1.0 / 6.0, 1.0 / 24.0, 1.0 / 120.0, 1.0 / 720.0, 1.0 / 5040.0)
 AHEAD = 2
 PP_BUFS = 4
 QB_BUFS = 1
-GP_BUFS = 3
+GP_BUFS = 2
 LOADS = ("w", "h0", "h1", "p0", "p1", "p2", "p3")
 H_COPY = "VSVS"
 Y_COPY = "SVSVSVSV"
-P_COPY = ("VS", "VS", "VS", "VS", "VV", "VV", "VV", "VV")
-Q_COPY = "VVVVVVVV"
+P_COPY = ("VS", "VS", "SS", "SS", "SS", "SS", "SS", "SS")
+Q_COPY = "VVSSSSSS"
 SCALE_ENG = "VVVVVVVV"
 LAST_SPLIT = 4
 A_ENG = "SSSSPPPP"
-G_FIN = "GGGGGGGG"
-G_CLAMP = False
 Y_MAX = math.sqrt((1.0 + ARG_MAX) / (1.0 - ARG_MAX))
 
 
@@ -85,12 +91,18 @@ def tile_hyperbolicuniform_pa_kernel(tc, h_mlp, W3, b3, prototypes, out_0, out_1
             return keep.tile([P, w], F32, name=name)
 
         ss, cs, xx, th, rx, sc = stat("ss"), stat("cs"), stat("xx"), stat("th"), stat("rx"), stat("sc")
+        zz, em = stat("zz"), stat("em")
         s2, bn, ee, be, rr, nr, omr = stat("s2"), stat("bn"), stat("ee"), stat("be"), stat("rr"), stat("nr"), stat("omr")
         a_g = [stat("a_g%d" % g, 4) for g in range(NG)]
         q_g = [stat("q_g%d" % g, 4) for g in range(NG)]
 
         h_sb = ring.tile([P, NT, H], BF16, name="h_sb", tag="y", bufs=Y_BUFS, align_bytes=64)
-        p_sb = [ring.tile([P, 8, D], BF16, name="p_sb%d" % k, tag="p_sb", bufs=4) for k in range(4)]
+        p_sb = {}
+
+        def p_load(k):
+            p_sb[k] = ring.tile([P, 4, D], BF16, name="p_sb", tag="p_sb", bufs=PS_BUFS)
+            nc.sync.dma_start(out=p_sb[k], in_=p_v[:, 4 * k : 4 * k + 4, :])
+
         for what in LOADS:
             if what == "w":
                 nc.sync.dma_start(out=w_raw, in_=w_v)
@@ -98,8 +110,7 @@ def tile_hyperbolicuniform_pa_kernel(tc, h_mlp, W3, b3, prototypes, out_0, out_1
                 k = int(what[1])
                 nc.sync.dma_start(out=h_sb[:, 4 * k : 4 * k + 4, :], in_=h_v[:, 4 * k : 4 * k + 4, :])
             else:
-                k = int(what[1])
-                nc.sync.dma_start(out=p_sb[k], in_=p_v[:, 8 * k : 8 * k + 8, :])
+                p_load(int(what[1]))
         nc.scalar.dma_start(out=b_bc, in_=b3.partition_broadcast(P))
         make_identity(nc, ident)
         nc.vector.memset(warm, 1.0)
@@ -161,8 +172,16 @@ def tile_hyperbolicuniform_pa_kernel(tc, h_mlp, W3, b3, prototypes, out_0, out_1
         def row_stats():
             nc.vector.tensor_scalar(out=cs, in0=ss, scalar1=C, scalar2=C * 1e-30, op0=ALU.mult, op1=ALU.max)
             nc.scalar.activation(out=xx, in_=cs, func=ACT.Sqrt)
-            nc.scalar.activation(out=th, in_=xx, func=ACT.Tanh)
             nc.vector.reciprocal(out=rx, in_=xx)
+            nc.vector.tensor_scalar(out=zz, in0=xx, scalar1=X_TOP, scalar2=2.0 / 2 ** DOUBLINGS, op0=ALU.min, op1=ALU.mult)
+            nc.vector.tensor_scalar(out=em, in0=zz, scalar1=INV_FACT[TERMS], scalar2=None, op0=ALU.mult)
+            for k in range(TERMS - 1, 0, -1):
+                nc.vector.scalar_tensor_tensor(out=em, in0=em, scalar=INV_FACT[k], in1=zz, op0=ALU.add, op1=ALU.mult)
+            for k in range(DOUBLINGS):
+                nc.vector.scalar_tensor_tensor(out=em, in0=em, scalar=2.0, in1=em, op0=ALU.add, op1=ALU.mult)
+            nc.vector.tensor_scalar(out=th, in0=em, scalar1=2.0, scalar2=None, op0=ALU.add)
+            nc.vector.reciprocal(out=th, in_=th)
+            nc.vector.tensor_tensor(out=th, in0=th, in1=em, op=ALU.mult)
             nc.vector.tensor_tensor(out=sc, in0=th, in1=rx, op=ALU.mult)
 
         def row_stats2():
@@ -208,7 +227,7 @@ def tile_hyperbolicuniform_pa_kernel(tc, h_mlp, W3, b3, prototypes, out_0, out_1
             ps = psum.tile([P, 2, 2, P], F32, name="tr_p", tag="tr", bufs=2)
             for a in range(2):
                 r = 4 * g + 2 * hb + a
-                words = p_sb[r // 8][:, r % 8, :].bitcast(F32)
+                words = p_sb[r // 4][:, r % 4, :].bitcast(F32)
                 for u in range(2):
                     nc.tensor.transpose(ps[:, a, u, :], words[:, P * u : P * u + P], ident)
             copy_out(
@@ -227,7 +246,7 @@ def tile_hyperbolicuniform_pa_kernel(tc, h_mlp, W3, b3, prototypes, out_0, out_1
 
         def p_norm(g, a):
             r = 4 * g + a
-            rows = p_sb[r // 8][:, r % 8, :]
+            rows = p_sb[r // 4][:, r % 4, :]
             if A_ENG[g] == "S":
                 nc.scalar.activation(out=junk_s, in_=rows, func=ACT.Square, accum_out=a_g[g][:, a : a + 1])
             else:
@@ -256,23 +275,33 @@ def tile_hyperbolicuniform_pa_kernel(tc, h_mlp, W3, b3, prototypes, out_0, out_1
                 nc.tensor.transpose(qb[:, P * a : P * a + P], q_g[g][:, a : a + 1].to_broadcast([P, P]), ident)
             copy_out(eng, q_sb[:, GRP * g : GRP * g + GRP], qb)
 
-        def p_group(g, e0="V", e1="S", e2="V"):
-            p_transpose(g, 0, e0)
-            p_transpose(g, 1, e1)
-            if A_ENG[g] == "P":
-                p_norm_pe(g)
+        def p_stage(g, stage):
+            if stage == 0:
+                p_transpose(g, 0, P_COPY[g][0])
+                p_transpose(g, 1, P_COPY[g][1])
+            elif stage == 1:
+                if A_ENG[g] == "P":
+                    p_norm_pe(g)
+                else:
+                    for a in range(4):
+                        p_norm(g, a)
+            elif stage == 2:
+                p_quant(g)
             else:
-                for a in range(4):
-                    p_norm(g, a)
-            p_quant(g)
-            p_factor(g, e2)
+                p_factor(g, Q_COPY[g])
+                if g + PS_BUFS < NG:
+                    p_load(g + PS_BUFS)
+
+        def p_group(g):
+            for stage in range(4):
+                p_stage(g, stage)
 
         t_tiles, y_tiles = {}, {}
 
         def products(b, g0, ng, t):
             rows = slice(P * t, P * t + P)
             tt = ring.tile([P, ng * GRP], F32, name="tt", tag="tt", bufs=T_BUFS, align_bytes=64)
-            t_tiles[(b, t)] = tt
+            t_tiles[(g0, t)] = tt
             for l in range(ng):
                 cols = slice(GRP * (g0 + l), GRP * (g0 + l) + GRP)
                 pp = psum.tile([P, GRP], F32, name="pp", tag="pp", bufs=PP_BUFS)
@@ -302,39 +331,27 @@ def tile_hyperbolicuniform_pa_kernel(tc, h_mlp, W3, b3, prototypes, out_0, out_1
             nc.gpsimd.tensor_scalar(out=z, in0=probe, scalar1=0.0, scalar2=0.0, op0=ALU.min, op1=ALU.max)
             return z
 
-        def roots(b, ng, t):
-            rr = gate_rr[b]
-            tt = t_tiles[(b, t)]
-            yy = ring.tile([P, ng * GRP], F32, name="yy", tag="y", bufs=Y_BUFS, align_bytes=64)
-            y_tiles[(b, t)] = yy
-            nc.scalar.activation(out=yy, in_=tt, func=ACT.Sqrt, scale=rr[:, t : t + 1], bias=nr[:, t : t + 1])
-            nc.scalar.activation(out=tt, in_=tt, func=ACT.Sqrt, scale=rr[:, t : t + 1], bias=omr[:, t : t + 1])
+        def y_part(b, b0, g0, ng, t):
+            return y_tiles[(b, t)][:, GRP * (g0 - b0) : GRP * (g0 - b0 + ng)]
 
-        def add_roots(b, t):
-            yy = y_tiles[(b, t)]
-            nc.vector.scalar_tensor_tensor(out=yy, in0=yy, scalar=0.0, in1=t_tiles[(b, t)], op0=ALU.max, op1=ALU.add)
-            if G_CLAMP:
-                nc.gpsimd.tensor_scalar(out=yy, in0=yy, scalar1=Y_MAX, scalar2=1.0, op0=ALU.min, op1=ALU.max)
+        def roots(b, b0, g0, ng, t):
+            rr_b = gate_rr[b]
+            tt = t_tiles[(g0, t)]
+            if (b, t) not in y_tiles:
+                y_tiles[(b, t)] = ring.tile([P, BLOCKS[b] * GRP], F32, name="yy", tag="y", bufs=Y_BUFS, align_bytes=64)
+            yy = y_part(b, b0, g0, ng, t)
+            nc.scalar.activation(out=yy, in_=tt, func=ACT.Sqrt, scale=rr_b[:, t : t + 1], bias=nr[:, t : t + 1])
+            nc.scalar.activation(out=tt, in_=tt, func=ACT.Sqrt, scale=rr_b[:, t : t + 1], bias=omr[:, t : t + 1])
 
-        def log_(b, t, part=None):
-            yy = y_tiles[(b, t)]
-            if part is not None:
-                yy = yy[:, part[0] : part[1]]
+        def add_roots(b, b0, g0, ng, t):
+            yy = y_part(b, b0, g0, ng, t)
+            nc.vector.scalar_tensor_tensor(out=yy, in0=yy, scalar=0.0, in1=t_tiles[(g0, t)], op0=ALU.max, op1=ALU.add)
+
+        def finish(b, b0, t, lo, hi):
+            yy = y_tiles[(b, t)][:, lo:hi]
             nc.scalar.activation(out=yy, in_=yy, func=ACT.Ln, bias=gate_ln[b])
-
-        def finish(b, g0, ng, t, part=None):
-            yy = y_tiles[(b, t)]
-            if part is not None:
-                yy = yy[:, part[0] : part[1]]
-                nc.vector.tensor_scalar(out=yy, in0=yy, scalar1=-K_OUT, scalar2=LOGIT_MIN, op0=ALU.mult, op1=ALU.max)
-                nc.sync.dma_start(out=lg_v[:, t, GRP * g0 + part[0] : GRP * g0 + part[1]], in_=yy)
-                return
-            k_out = -K_OUT
-            if G_CLAMP and G_FIN[t] == "G":
-                nc.gpsimd.tensor_scalar(out=yy, in0=yy, scalar1=k_out, scalar2=0.0, op0=ALU.mult, op1=ALU.add)
-            else:
-                nc.vector.tensor_scalar(out=yy, in0=yy, scalar1=k_out, scalar2=LOGIT_MIN, op0=ALU.mult, op1=ALU.max)
-            nc.sync.dma_start(out=lg_v[:, t, GRP * g0 : GRP * (g0 + ng)], in_=yy)
+            nc.vector.tensor_scalar(out=yy, in0=yy, scalar1=-K_OUT, scalar2=LOGIT_MIN, op0=ALU.mult, op1=ALU.max)
+            nc.sync.dma_start(out=lg_v[:, t, GRP * b0 + lo : GRP * b0 + hi], in_=yy)
 
         w3_prep()
         h_transpose(0, H_COPY[0])
@@ -353,33 +370,37 @@ def tile_hyperbolicuniform_pa_kernel(tc, h_mlp, W3, b3, prototypes, out_0, out_1
                 nc.sync.dma_start(out=hy_v[:, t - 3 : t + 1, :], in_=hy[t // 4])
                 hyp_quant(t // 4)
         row_stats2()
-        for g in range(BLOCKS[0]):
-            p_group(g, P_COPY[g][0], P_COPY[g][1], Q_COPY[g])
-
-        g0 = 0
-        for b, ng in enumerate(BLOCKS):
+        passes = []
+        b0 = 0
+        for b, nb in enumerate(BLOCKS):
+            for g0 in range(b0, b0 + nb, SUB):
+                passes.append((b, b0, g0, min(SUB, b0 + nb - g0)))
+            b0 += nb
+        for g in range(passes[0][3]):
+            p_group(g)
+        for k, (b, b0, g0, ng) in enumerate(passes):
             for t in range(min(AHEAD, NT)):
                 products(b, g0, ng, t)
+            last_of_block = k + 1 == len(passes) or passes[k + 1][0] != b
+            todo = [] if last_of_block else [(g, s) for g in range(g0 + ng, g0 + ng + passes[k + 1][3]) for s in range(4)]
             for t in range(NT):
-                roots(b, ng, t)
+                roots(b, b0, g0, ng, t)
                 if t + AHEAD < NT:
                     products(b, g0, ng, t + AHEAD)
-                add_roots(b, t)
-            gate_ln[b] = gate("gate_ln%d" % b, t_tiles[(b, NT - 1)][:, 0:1])
+                add_roots(b, b0, g0, ng, t)
+                for g, s in todo[len(todo) * t // PREP_T : len(todo) * (t + 1) // PREP_T]:
+                    p_stage(g, s)
+            if not last_of_block:
+                continue
+            gate_ln[b] = gate("gate_ln%d" % b, t_tiles[(g0, NT - 1)][:, 0:1])
+            width = BLOCKS[b] * GRP
             for t in range(NT):
-                if t == NT - 1 and b + 1 == len(BLOCKS) and LAST_SPLIT > 1:
-                    w = ng * GRP // LAST_SPLIT
-                    for k in range(LAST_SPLIT):
-                        log_(b, t, (w * k, w * k + w))
-                        finish(b, g0, ng, t, (w * k, w * k + w))
-                    continue
-                log_(b, t)
-                if t == NT - 1 and b + 1 < len(BLOCKS):
-                    z = gate("gate_z%d" % b, y_tiles[(b, t)][:, 0:1])
-                    gate_rr[b + 1] = stat("rr%d" % (b + 1))
-                    nc.gpsimd.tensor_scalar(out=gate_rr[b + 1], in0=rr, scalar1=z, scalar2=0.0, op0=ALU.add, op1=ALU.add)
-                finish(b, g0, ng, t)
-            if b + 1 < len(BLOCKS):
-                for g in range(g0 + ng, g0 + ng + BLOCKS[b + 1]):
-                    p_group(g, P_COPY[g][0], P_COPY[g][1], Q_COPY[g])
-            g0 += ng
+                step = LN_W if (t < NT - 1 or k + 1 < len(passes)) else LN_W // LAST_SPLIT
+                for lo in range(0, width, step):
+                    finish(b, b0, t, lo, min(lo + step, width))
+            if k + 1 < len(passes):
+                z = gate("gate_z%d" % b, y_tiles[(b, NT - 1)][:, width - 1 : width])
+                gate_rr[b + 1] = stat("rr%d" % (b + 1))
+                nc.gpsimd.tensor_scalar(out=gate_rr[b + 1], in0=rr, scalar1=z, scalar2=0.0, op0=ALU.add, op1=ALU.add)
+                for g in range(g0 + ng, g0 + ng + passes[k + 1][3]):
+                    p_group(g)

@@ -26,30 +26,24 @@ EDGE = 1e-6
 
 FLOPS = 2 * B * H * D + 2 * B * N * D
 
-BLOCKS = (8,)
-SUB = 4
-LN_W = 1024
-PS_BUFS = 4
-PREP_T = 6
-T_BUFS = 3
-Y_BUFS = 8
+BLOCKS = (3, 3, 2)
+T_BUFS = 5
+Y_BUFS = 10
 MANUAL = False
-X_TOP = 16.0
-DOUBLINGS = 8
-TERMS = 7
-INV_FACT = (1.0, 1.0, 1.0 / 2.0, 1.0 / 6.0, 1.0 / 24.0, 1.0 / 120.0, 1.0 / 720.0, 1.0 / 5040.0)
 AHEAD = 2
 PP_BUFS = 4
 QB_BUFS = 1
-GP_BUFS = 2
+GP_BUFS = 3
 LOADS = ("w", "h0", "h1", "p0", "p1", "p2", "p3")
 H_COPY = "VSVS"
 Y_COPY = "SVSVSVSV"
-P_COPY = ("VS", "VS", "SS", "SS", "SS", "SS", "SS", "SS")
-Q_COPY = "VVSSSSSS"
+P_COPY = ("VS", "VS", "VS", "VS", "VV", "VV", "VV", "VV")
+Q_COPY = "VVVVVVVV"
 SCALE_ENG = "VVVVVVVV"
 LAST_SPLIT = 4
 A_ENG = "SSSSPPPP"
+G_FIN = "GGGGGGGG"
+G_CLAMP = False
 Y_MAX = math.sqrt((1.0 + ARG_MAX) / (1.0 - ARG_MAX))
 
 
@@ -86,23 +80,18 @@ def tile_hyperbolicuniform_pa_kernel(tc, h_mlp, W3, b3, prototypes, out_0, out_1
         junk_d = keep.tile([P, P], F32, name="junk_d")
         warm = keep.tile([P, 1], F32, name="warm")
         warm2 = keep.tile([P, 1], F32, name="warm2")
+        zero = keep.tile([P, 1], F32, name="zero")
 
         def stat(name, w=NT):
             return keep.tile([P, w], F32, name=name)
 
         ss, cs, xx, th, rx, sc = stat("ss"), stat("cs"), stat("xx"), stat("th"), stat("rx"), stat("sc")
-        zz, em = stat("zz"), stat("em")
         s2, bn, ee, be, rr, nr, omr = stat("s2"), stat("bn"), stat("ee"), stat("be"), stat("rr"), stat("nr"), stat("omr")
         a_g = [stat("a_g%d" % g, 4) for g in range(NG)]
         q_g = [stat("q_g%d" % g, 4) for g in range(NG)]
 
         h_sb = ring.tile([P, NT, H], BF16, name="h_sb", tag="y", bufs=Y_BUFS, align_bytes=64)
-        p_sb = {}
-
-        def p_load(k):
-            p_sb[k] = ring.tile([P, 4, D], BF16, name="p_sb", tag="p_sb", bufs=PS_BUFS)
-            nc.sync.dma_start(out=p_sb[k], in_=p_v[:, 4 * k : 4 * k + 4, :])
-
+        p_sb = [ring.tile([P, 8, D], BF16, name="p_sb%d" % k, tag="p_sb", bufs=4) for k in range(4)]
         for what in LOADS:
             if what == "w":
                 nc.sync.dma_start(out=w_raw, in_=w_v)
@@ -110,10 +99,12 @@ def tile_hyperbolicuniform_pa_kernel(tc, h_mlp, W3, b3, prototypes, out_0, out_1
                 k = int(what[1])
                 nc.sync.dma_start(out=h_sb[:, 4 * k : 4 * k + 4, :], in_=h_v[:, 4 * k : 4 * k + 4, :])
             else:
-                p_load(int(what[1]))
+                k = int(what[1])
+                nc.sync.dma_start(out=p_sb[k], in_=p_v[:, 8 * k : 8 * k + 8, :])
         nc.scalar.dma_start(out=b_bc, in_=b3.partition_broadcast(P))
         make_identity(nc, ident)
         nc.vector.memset(warm, 1.0)
+        nc.vector.memset(zero, 0.0)
         nc.scalar.activation(out=warm2, in_=warm, func=ACT.Sqrt)
 
         def copy_out(eng, out, in_):
@@ -172,16 +163,8 @@ def tile_hyperbolicuniform_pa_kernel(tc, h_mlp, W3, b3, prototypes, out_0, out_1
         def row_stats():
             nc.vector.tensor_scalar(out=cs, in0=ss, scalar1=C, scalar2=C * 1e-30, op0=ALU.mult, op1=ALU.max)
             nc.scalar.activation(out=xx, in_=cs, func=ACT.Sqrt)
+            nc.scalar.activation(out=th, in_=xx, func=ACT.Tanh)
             nc.vector.reciprocal(out=rx, in_=xx)
-            nc.vector.tensor_scalar(out=zz, in0=xx, scalar1=X_TOP, scalar2=2.0 / 2 ** DOUBLINGS, op0=ALU.min, op1=ALU.mult)
-            nc.vector.tensor_scalar(out=em, in0=zz, scalar1=INV_FACT[TERMS], scalar2=None, op0=ALU.mult)
-            for k in range(TERMS - 1, 0, -1):
-                nc.vector.scalar_tensor_tensor(out=em, in0=em, scalar=INV_FACT[k], in1=zz, op0=ALU.add, op1=ALU.mult)
-            for k in range(DOUBLINGS):
-                nc.vector.scalar_tensor_tensor(out=em, in0=em, scalar=2.0, in1=em, op0=ALU.add, op1=ALU.mult)
-            nc.vector.tensor_scalar(out=th, in0=em, scalar1=2.0, scalar2=None, op0=ALU.add)
-            nc.vector.reciprocal(out=th, in_=th)
-            nc.vector.tensor_tensor(out=th, in0=th, in1=em, op=ALU.mult)
             nc.vector.tensor_tensor(out=sc, in0=th, in1=rx, op=ALU.mult)
 
         def row_stats2():
@@ -227,7 +210,7 @@ def tile_hyperbolicuniform_pa_kernel(tc, h_mlp, W3, b3, prototypes, out_0, out_1
             ps = psum.tile([P, 2, 2, P], F32, name="tr_p", tag="tr", bufs=2)
             for a in range(2):
                 r = 4 * g + 2 * hb + a
-                words = p_sb[r // 4][:, r % 4, :].bitcast(F32)
+                words = p_sb[r // 8][:, r % 8, :].bitcast(F32)
                 for u in range(2):
                     nc.tensor.transpose(ps[:, a, u, :], words[:, P * u : P * u + P], ident)
             copy_out(
@@ -246,7 +229,7 @@ def tile_hyperbolicuniform_pa_kernel(tc, h_mlp, W3, b3, prototypes, out_0, out_1
 
         def p_norm(g, a):
             r = 4 * g + a
-            rows = p_sb[r // 4][:, r % 4, :]
+            rows = p_sb[r // 8][:, r % 8, :]
             if A_ENG[g] == "S":
                 nc.scalar.activation(out=junk_s, in_=rows, func=ACT.Square, accum_out=a_g[g][:, a : a + 1])
             else:
@@ -275,33 +258,23 @@ def tile_hyperbolicuniform_pa_kernel(tc, h_mlp, W3, b3, prototypes, out_0, out_1
                 nc.tensor.transpose(qb[:, P * a : P * a + P], q_g[g][:, a : a + 1].to_broadcast([P, P]), ident)
             copy_out(eng, q_sb[:, GRP * g : GRP * g + GRP], qb)
 
-        def p_stage(g, stage):
-            if stage == 0:
-                p_transpose(g, 0, P_COPY[g][0])
-                p_transpose(g, 1, P_COPY[g][1])
-            elif stage == 1:
-                if A_ENG[g] == "P":
-                    p_norm_pe(g)
-                else:
-                    for a in range(4):
-                        p_norm(g, a)
-            elif stage == 2:
-                p_quant(g)
+        def p_group(g, e0="V", e1="S", e2="V"):
+            p_transpose(g, 0, e0)
+            p_transpose(g, 1, e1)
+            if A_ENG[g] == "P":
+                p_norm_pe(g)
             else:
-                p_factor(g, Q_COPY[g])
-                if g + PS_BUFS < NG:
-                    p_load(g + PS_BUFS)
-
-        def p_group(g):
-            for stage in range(4):
-                p_stage(g, stage)
+                for a in range(4):
+                    p_norm(g, a)
+            p_quant(g)
+            p_factor(g, e2)
 
         t_tiles, y_tiles = {}, {}
 
         def products(b, g0, ng, t):
             rows = slice(P * t, P * t + P)
             tt = ring.tile([P, ng * GRP], F32, name="tt", tag="tt", bufs=T_BUFS, align_bytes=64)
-            t_tiles[(g0, t)] = tt
+            t_tiles[(b, t)] = tt
             for l in range(ng):
                 cols = slice(GRP * (g0 + l), GRP * (g0 + l) + GRP)
                 pp = psum.tile([P, GRP], F32, name="pp", tag="pp", bufs=PP_BUFS)
@@ -326,32 +299,45 @@ def tile_hyperbolicuniform_pa_kernel(tc, h_mlp, W3, b3, prototypes, out_0, out_1
         gate_rr = {0: rr}
         gate_ln = {}
 
-        def gate(name, probe):
-            z = keep.tile([P, 1], F32, name=name)
-            nc.gpsimd.tensor_scalar(out=z, in0=probe, scalar1=0.0, scalar2=0.0, op0=ALU.min, op1=ALU.max)
+        def gate(name, probe, value):
+            z = keep.tile([P, value.shape[1]], F32, name=name)
+            nc.scalar.copy(out=z[:, 0:1], in_=probe)
+            nc.scalar.copy(out=z, in_=value)
             return z
 
-        def y_part(b, b0, g0, ng, t):
-            return y_tiles[(b, t)][:, GRP * (g0 - b0) : GRP * (g0 - b0 + ng)]
+        def roots(b, ng, t):
+            rr = gate_rr[b]
+            tt = t_tiles[(b, t)]
+            yy = ring.tile([P, ng * GRP], F32, name="yy", tag="y", bufs=Y_BUFS, align_bytes=64)
+            y_tiles[(b, t)] = yy
+            nc.scalar.activation(out=yy, in_=tt, func=ACT.Sqrt, scale=rr[:, t : t + 1], bias=nr[:, t : t + 1])
+            nc.scalar.activation(out=tt, in_=tt, func=ACT.Sqrt, scale=rr[:, t : t + 1], bias=omr[:, t : t + 1])
 
-        def roots(b, b0, g0, ng, t):
-            rr_b = gate_rr[b]
-            tt = t_tiles[(g0, t)]
-            if (b, t) not in y_tiles:
-                y_tiles[(b, t)] = ring.tile([P, BLOCKS[b] * GRP], F32, name="yy", tag="y", bufs=Y_BUFS, align_bytes=64)
-            yy = y_part(b, b0, g0, ng, t)
-            nc.scalar.activation(out=yy, in_=tt, func=ACT.Sqrt, scale=rr_b[:, t : t + 1], bias=nr[:, t : t + 1])
-            nc.scalar.activation(out=tt, in_=tt, func=ACT.Sqrt, scale=rr_b[:, t : t + 1], bias=omr[:, t : t + 1])
+        def add_roots(b, t):
+            yy = y_tiles[(b, t)]
+            nc.vector.scalar_tensor_tensor(out=yy, in0=yy, scalar=0.0, in1=t_tiles[(b, t)], op0=ALU.max, op1=ALU.add)
+            if G_CLAMP:
+                nc.gpsimd.tensor_scalar(out=yy, in0=yy, scalar1=Y_MAX, scalar2=1.0, op0=ALU.min, op1=ALU.max)
 
-        def add_roots(b, b0, g0, ng, t):
-            yy = y_part(b, b0, g0, ng, t)
-            nc.vector.scalar_tensor_tensor(out=yy, in0=yy, scalar=0.0, in1=t_tiles[(g0, t)], op0=ALU.max, op1=ALU.add)
-
-        def finish(b, b0, t, lo, hi):
-            yy = y_tiles[(b, t)][:, lo:hi]
+        def log_(b, t, part=None):
+            yy = y_tiles[(b, t)]
+            if part is not None:
+                yy = yy[:, part[0] : part[1]]
             nc.scalar.activation(out=yy, in_=yy, func=ACT.Ln, bias=gate_ln[b])
-            nc.vector.tensor_scalar(out=yy, in0=yy, scalar1=-K_OUT, scalar2=LOGIT_MIN, op0=ALU.mult, op1=ALU.max)
-            nc.sync.dma_start(out=lg_v[:, t, GRP * b0 + lo : GRP * b0 + hi], in_=yy)
+
+        def finish(b, g0, ng, t, part=None):
+            yy = y_tiles[(b, t)]
+            if part is not None:
+                yy = yy[:, part[0] : part[1]]
+                nc.vector.tensor_scalar(out=yy, in0=yy, scalar1=-K_OUT, scalar2=LOGIT_MIN, op0=ALU.mult, op1=ALU.max)
+                nc.sync.dma_start(out=lg_v[:, t, GRP * g0 + part[0] : GRP * g0 + part[1]], in_=yy)
+                return
+            k_out = -K_OUT
+            if G_CLAMP and G_FIN[t] == "G":
+                nc.gpsimd.tensor_scalar(out=yy, in0=yy, scalar1=k_out, scalar2=0.0, op0=ALU.mult, op1=ALU.add)
+            else:
+                nc.vector.tensor_scalar(out=yy, in0=yy, scalar1=k_out, scalar2=LOGIT_MIN, op0=ALU.mult, op1=ALU.max)
+            nc.sync.dma_start(out=lg_v[:, t, GRP * g0 : GRP * (g0 + ng)], in_=yy)
 
         w3_prep()
         h_transpose(0, H_COPY[0])
@@ -370,37 +356,31 @@ def tile_hyperbolicuniform_pa_kernel(tc, h_mlp, W3, b3, prototypes, out_0, out_1
                 nc.sync.dma_start(out=hy_v[:, t - 3 : t + 1, :], in_=hy[t // 4])
                 hyp_quant(t // 4)
         row_stats2()
-        passes = []
-        b0 = 0
-        for b, nb in enumerate(BLOCKS):
-            for g0 in range(b0, b0 + nb, SUB):
-                passes.append((b, b0, g0, min(SUB, b0 + nb - g0)))
-            b0 += nb
-        for g in range(passes[0][3]):
-            p_group(g)
-        for k, (b, b0, g0, ng) in enumerate(passes):
+        for g in range(BLOCKS[0]):
+            p_group(g, P_COPY[g][0], P_COPY[g][1], Q_COPY[g])
+
+        g0 = 0
+        for b, ng in enumerate(BLOCKS):
             for t in range(min(AHEAD, NT)):
                 products(b, g0, ng, t)
-            last_of_block = k + 1 == len(passes) or passes[k + 1][0] != b
-            todo = [] if last_of_block else [(g, s) for g in range(g0 + ng, g0 + ng + passes[k + 1][3]) for s in range(4)]
             for t in range(NT):
-                roots(b, b0, g0, ng, t)
+                roots(b, ng, t)
                 if t + AHEAD < NT:
                     products(b, g0, ng, t + AHEAD)
-                add_roots(b, b0, g0, ng, t)
-                for g, s in todo[len(todo) * t // PREP_T : len(todo) * (t + 1) // PREP_T]:
-                    p_stage(g, s)
-            if not last_of_block:
-                continue
-            gate_ln[b] = gate("gate_ln%d" % b, t_tiles[(g0, NT - 1)][:, 0:1])
-            width = BLOCKS[b] * GRP
+                add_roots(b, t)
+            gate_ln[b] = gate("gate_ln%d" % b, t_tiles[(b, NT - 1)][:, 0:1], zero)
             for t in range(NT):
-                step = LN_W if (t < NT - 1 or k + 1 < len(passes)) else LN_W // LAST_SPLIT
-                for lo in range(0, width, step):
-                    finish(b, b0, t, lo, min(lo + step, width))
-            if k + 1 < len(passes):
-                z = gate("gate_z%d" % b, y_tiles[(b, NT - 1)][:, width - 1 : width])
-                gate_rr[b + 1] = stat("rr%d" % (b + 1))
-                nc.gpsimd.tensor_scalar(out=gate_rr[b + 1], in0=rr, scalar1=z, scalar2=0.0, op0=ALU.add, op1=ALU.add)
-                for g in range(g0 + ng, g0 + ng + passes[k + 1][3]):
-                    p_group(g)
+                if t == NT - 1 and b + 1 == len(BLOCKS) and LAST_SPLIT > 1:
+                    w = ng * GRP // LAST_SPLIT
+                    for k in range(LAST_SPLIT):
+                        log_(b, t, (w * k, w * k + w))
+                        finish(b, g0, ng, t, (w * k, w * k + w))
+                    continue
+                log_(b, t)
+                if t == NT - 1 and b + 1 < len(BLOCKS):
+                    gate_rr[b + 1] = gate("gate_rr%d" % (b + 1), y_tiles[(b, t)][:, 0:1], rr)
+                finish(b, g0, ng, t)
+            if b + 1 < len(BLOCKS):
+                for g in range(g0 + ng, g0 + ng + BLOCKS[b + 1]):
+                    p_group(g, P_COPY[g][0], P_COPY[g][1], Q_COPY[g])
+            g0 += ng

import math
from contextlib import ExitStack

import concourse.mybir as mybir
from concourse.masks import make_identity

F32 = mybir.dt.float32
BF16 = mybir.dt.bfloat16
U32 = mybir.dt.uint32
U8 = mybir.dt.uint8
FP8X4 = mybir.dt.float8_e4m3fn_x4
ALU = mybir.AluOpType
ACT = mybir.ActivationFunctionType

P = 128
B, H, D, N = 1024, 512, 512, 4096
NT = B // P
GRP = 512
NG = N // GRP
C = 3.0
TEMP = 0.07
K_OUT = 2.0 / (math.sqrt(C) * TEMP)
ARG_MAX = 1.0 - 1e-5
LOGIT_MIN = -(1.0 / (math.sqrt(C) * TEMP)) * math.log((1.0 + ARG_MAX) / (1.0 - ARG_MAX))
EDGE = 1e-6

FLOPS = 2 * B * H * D + 2 * B * N * D

BLOCKS = (3, 3, 2)
T_BUFS = 5
Y_BUFS = 10
MANUAL = False
AHEAD = 2
PP_BUFS = 4
QB_BUFS = 1
GP_BUFS = 3
LOADS = ("w", "h0", "h1", "p0", "p1", "p2", "p3")
H_COPY = "VSVS"
Y_COPY = "SVSVSVSV"
P_COPY = ("VS", "VS", "VS", "VS", "VV", "VV", "VV", "VV")
Q_COPY = "VVVVVVVV"
SCALE_ENG = "VVVVVVVV"
LAST_SPLIT = 4
A_ENG = "SSSSPPPP"
G_FIN = "GGGGGGGG"
G_CLAMP = False
Y_MAX = math.sqrt((1.0 + ARG_MAX) / (1.0 - ARG_MAX))


def tile_hyperbolicuniform_pa_kernel(tc, h_mlp, W3, b3, prototypes, out_0, out_1):
    nc = tc.nc
    with ExitStack() as ctx:
        if MANUAL:
            ctx.enter_context(tc.manual_schedule())
        keep = ctx.enter_context(tc.tile_pool(name="keep", bufs=1))
        ring = ctx.enter_context(tc.tile_pool(name="ring", bufs=1))
        psum = ctx.enter_context(tc.psum_pool(name="psum", bufs=1))

        h_v = h_mlp.rearrange("(p t) k -> p t k", t=NT)
        w_v = W3.rearrange("(u q e) c -> q u (e c)", u=2, e=2)
        p_v = prototypes.rearrange("(r p) d -> p r d", p=P)
        lg_v = out_0.rearrange("(p t) j -> p t j", t=NT)
        hy_v = out_1.rearrange("(p t) d -> p t d", t=NT)

        ident = keep.tile([P, P], F32, name="ident")
        b_bc = keep.tile([P, D], BF16, name="b_bc")
        w_raw = ring.tile([P, 2, 2 * D], BF16, name="w_raw", tag="tt", bufs=T_BUFS, align_bytes=64)
        w_grp = ring.tile([P, D, 4], BF16, name="w_grp", tag="tt", bufs=T_BUFS, align_bytes=64)
        w_codes = keep.tile([P, D], U32, name="w_codes", align_bytes=64)
        w_scales = keep.tile([P, D], U8, name="w_scales", align_bytes=64)
        h_codes = keep.tile([P, B], U32, name="h_codes", align_bytes=64)
        h_scales = keep.tile([P, B], U8, name="h_scales", align_bytes=64)
        y_codes = keep.tile([P, B], U32, name="y_codes", align_bytes=64)
        y_scales = keep.tile([P, B], U8, name="y_scales", align_bytes=64)
        p_codes = keep.tile([P, N], U32, name="p_codes", align_bytes=64)
        p_scales = keep.tile([P, N], U8, name="p_scales", align_bytes=64)
        q_sb = keep.tile([P, N], F32, name="q_sb")
        junk_s = keep.tile([P, D], BF16, name="junk_s")
        junk_v = keep.tile([P, D], F32, name="junk_v") if "V" in A_ENG else None
        junk_d = keep.tile([P, P], F32, name="junk_d")
        warm = keep.tile([P, 1], F32, name="warm")
        warm2 = keep.tile([P, 1], F32, name="warm2")
        zero = keep.tile([P, 1], F32, name="zero")

        def stat(name, w=NT):
            return keep.tile([P, w], F32, name=name)

        ss, cs, xx, th, rx, sc = stat("ss"), stat("cs"), stat("xx"), stat("th"), stat("rx"), stat("sc")
        s2, bn, ee, be, rr, nr, omr = stat("s2"), stat("bn"), stat("ee"), stat("be"), stat("rr"), stat("nr"), stat("omr")
        a_g = [stat("a_g%d" % g, 4) for g in range(NG)]
        q_g = [stat("q_g%d" % g, 4) for g in range(NG)]

        h_sb = ring.tile([P, NT, H], BF16, name="h_sb", tag="y", bufs=Y_BUFS, align_bytes=64)
        p_sb = [ring.tile([P, 8, D], BF16, name="p_sb%d" % k, tag="p_sb", bufs=4) for k in range(4)]
        for what in LOADS:
            if what == "w":
                nc.sync.dma_start(out=w_raw, in_=w_v)
            elif what[0] == "h":
                k = int(what[1])
                nc.sync.dma_start(out=h_sb[:, 4 * k : 4 * k + 4, :], in_=h_v[:, 4 * k : 4 * k + 4, :])
            else:
                k = int(what[1])
                nc.sync.dma_start(out=p_sb[k], in_=p_v[:, 8 * k : 8 * k + 8, :])
        nc.scalar.dma_start(out=b_bc, in_=b3.partition_broadcast(P))
        make_identity(nc, ident)
        nc.vector.memset(warm, 1.0)
        nc.vector.memset(zero, 0.0)
        nc.scalar.activation(out=warm2, in_=warm, func=ACT.Sqrt)

        def copy_out(eng, out, in_):
            if eng == "V":
                nc.vector.tensor_copy(out=out, in_=in_)
            else:
                nc.scalar.copy(out=out, in_=in_)

        def w3_prep():
            nc.vector.tensor_copy(
                out=w_grp.rearrange("p (c i) t -> p c t i", i=4),
                in_=w_raw.rearrange("p u (e c i) -> p c (u e) i", e=2, i=4),
            )
            nc.vector.quantize_mx(out=w_codes.bitcast(FP8X4), scales=w_scales, in_=w_grp.rearrange("p c t -> p (c t)"))

        g_h = ring.tile([P, B, 2], F32, name="g_h", tag="y", bufs=Y_BUFS, align_bytes=64)

        def h_transpose(tp, eng):
            ps = psum.tile([P, 2, 2, P], F32, name="tr_h", tag="pp", bufs=PP_BUFS)
            for a in range(2):
                words = h_sb[:, 2 * tp + a, :].bitcast(F32)
                for u in range(2):
                    nc.tensor.transpose(ps[:, a, u, :], words[:, P * u : P * u + P], ident)
            copy_out(
                eng,
                g_h[:, 2 * P * tp : 2 * P * tp + 2 * P, :].rearrange("p (a i) u -> p a i u", a=2),
                ps.rearrange("p a u i -> p a i u"),
            )

        def h_quant(hf):
            cols = slice(512 * hf, 512 * hf + 512)
            nc.vector.quantize_mx(
                out=h_codes[:, cols].bitcast(FP8X4),
                scales=h_scales[:, cols],
                in_=g_h[:, cols, :].rearrange("p i u -> p (i u)").bitcast(BF16),
            )

        hy = [ring.tile([P, 4, D], F32, name="hy%d" % hf, tag="y", bufs=Y_BUFS, align_bytes=64) for hf in range(2)]

        def u_tile(t):
            rows = slice(P * t, P * t + P)
            u_ps = psum.tile([P, D], F32, name="u_ps", tag="pp", bufs=PP_BUFS)
            nc.tensor.matmul_mx(
                out=u_ps,
                lhsT=h_codes[:, rows].bitcast(FP8X4),
                lhsT_scale=h_scales[:, rows],
                rhs=w_codes.bitcast(FP8X4),
                rhs_scale=w_scales,
                start=True,
                stop=True,
            )
            ub = hy[t // 4][:, t % 4, :]
            nc.vector.tensor_tensor(out=ub, in0=u_ps, in1=b_bc, op=ALU.add)
            nc.scalar.activation(out=junk_s, in_=ub, func=ACT.Square, accum_out=ss[:, t : t + 1])

        def row_stats():
            nc.vector.tensor_scalar(out=cs, in0=ss, scalar1=C, scalar2=C * 1e-30, op0=ALU.mult, op1=ALU.max)
            nc.scalar.activation(out=xx, in_=cs, func=ACT.Sqrt)
            nc.scalar.activation(out=th, in_=xx, func=ACT.Tanh)
            nc.vector.reciprocal(out=rx, in_=xx)
            nc.vector.tensor_tensor(out=sc, in0=th, in1=rx, op=ALU.mult)

        def row_stats2():
            nc.vector.tensor_tensor(out=s2, in0=sc, in1=sc, op=ALU.mult)
            nc.vector.tensor_tensor(out=bn, in0=s2, in1=ss, op=ALU.mult)
            nc.vector.tensor_scalar(out=ee, in0=bn, scalar1=1.0 / C, scalar2=0.5, op0=ALU.add, op1=ALU.mult)
            nc.vector.tensor_scalar(out=be, in0=bn, scalar1=-C, scalar2=1.0, op0=ALU.mult, op1=ALU.add)
            nc.vector.tensor_scalar(out=be, in0=be, scalar1=EDGE, scalar2=None, op0=ALU.max)
            nc.vector.reciprocal(out=rr, in_=be)
            nc.vector.tensor_scalar(out=nr, in0=rr, scalar1=-1.0, scalar2=None, op0=ALU.mult)
            nc.vector.tensor_scalar(out=omr, in0=rr, scalar1=-1.0, scalar2=1.0, op0=ALU.mult, op1=ALU.add)

        g_y = ring.tile([P, B, 4], BF16, name="g_y", tag="y", bufs=Y_BUFS, align_bytes=64)

        def hyp_scale(t):
            ub = hy[t // 4][:, t % 4, :]
            if SCALE_ENG[t] == "V":
                nc.vector.tensor_scalar(out=ub, in0=ub, scalar1=sc[:, t : t + 1], scalar2=None, op0=ALU.mult)
            else:
                nc.scalar.activation(out=ub, in_=ub, func=ACT.Copy, scale=sc[:, t : t + 1])

        def hyp_transpose(t, eng):
            src = hy[t // 4][:, t % 4, :].rearrange("p (u m e) -> p u e m", u=2, e=2)
            ps = psum.tile([P, 4, P], F32, name="tr_y", tag="pp", bufs=PP_BUFS)
            for u in range(2):
                for e in range(2):
                    nc.tensor.transpose(ps[:, 2 * u + e, :], src[:, u, e, :], ident)
            copy_out(eng, g_y[:, P * t : P * t + P, :], ps.rearrange("p t i -> p i t"))

        def hyp_quant(hf):
            cols = slice(512 * hf, 512 * hf + 512)
            nc.vector.quantize_mx(
                out=y_codes[:, cols].bitcast(FP8X4),
                scales=y_scales[:, cols],
                in_=g_y[:, cols, :].rearrange("p i t -> p (i t)"),
            )

        g_p = {}

        def p_transpose(g, hb, eng):
            if hb == 0:
                g_p[g] = ring.tile([P, GRP, 2], F32, name="g_p", tag="g_p", bufs=GP_BUFS, align_bytes=64)
            ps = psum.tile([P, 2, 2, P], F32, name="tr_p", tag="tr", bufs=2)
            for a in range(2):
                r = 4 * g + 2 * hb + a
                words = p_sb[r // 8][:, r % 8, :].bitcast(F32)
                for u in range(2):
                    nc.tensor.transpose(ps[:, a, u, :], words[:, P * u : P * u + P], ident)
            copy_out(
                eng,
                g_p[g][:, 2 * P * hb : 2 * P * hb + 2 * P, :].rearrange("p (a j) u -> p a j u", a=2),
                ps.rearrange("p a u j -> p a j u"),
            )

        def p_quant(g):
            cols = slice(GRP * g, GRP * g + GRP)
            nc.vector.quantize_mx(
                out=p_codes[:, cols].bitcast(FP8X4),
                scales=p_scales[:, cols],
                in_=g_p[g].rearrange("p j u -> p (j u)").bitcast(BF16),
            )

        def p_norm(g, a):
            r = 4 * g + a
            rows = p_sb[r // 8][:, r % 8, :]
            if A_ENG[g] == "S":
                nc.scalar.activation(out=junk_s, in_=rows, func=ACT.Square, accum_out=a_g[g][:, a : a + 1])
            else:
                nc.vector.scalar_tensor_tensor(
                    out=junk_v, in0=rows, scalar=1.0, in1=rows, op0=ALU.mult, op1=ALU.mult, accum_out=a_g[g][:, a : a + 1]
                )

        def p_norm_pe(g):
            ga = psum.tile([P, 4, P], F32, name="ga", tag="ga", bufs=1)
            vals = g_p[g].rearrange("p j u -> p (j u)").bitcast(BF16).rearrange("p (j t) -> p j t", t=4)
            for a in range(4):
                for t in range(4):
                    cols = vals[:, P * a : P * a + P, t]
                    nc.tensor.matmul(out=ga[:, a, :], lhsT=cols, rhs=cols, start=(t == 0), stop=(t == 3))
            for a in range(4):
                nc.vector.scalar_tensor_tensor(
                    out=junk_d, in0=ga[:, a, :], scalar=1.0, in1=ident, op0=ALU.mult, op1=ALU.mult, accum_out=a_g[g][:, a : a + 1]
                )

        def p_factor(g, eng):
            nc.vector.tensor_scalar(out=q_g[g], in0=a_g[g], scalar1=(1.0 - EDGE) / C, scalar2=0.5, op0=ALU.min, op1=ALU.mult)
            nc.vector.tensor_scalar(out=q_g[g], in0=q_g[g], scalar1=-0.5 / C, scalar2=None, op0=ALU.add)
            nc.vector.reciprocal(out=q_g[g], in_=q_g[g])
            qb = psum.tile([P, GRP], F32, name="qb", tag="qb", bufs=QB_BUFS)
            for a in range(4):
                nc.tensor.transpose(qb[:, P * a : P * a + P], q_g[g][:, a : a + 1].to_broadcast([P, P]), ident)
            copy_out(eng, q_sb[:, GRP * g : GRP * g + GRP], qb)

        def p_group(g, e0="V", e1="S", e2="V"):
            p_transpose(g, 0, e0)
            p_transpose(g, 1, e1)
            if A_ENG[g] == "P":
                p_norm_pe(g)
            else:
                for a in range(4):
                    p_norm(g, a)
            p_quant(g)
            p_factor(g, e2)

        t_tiles, y_tiles = {}, {}

        def products(b, g0, ng, t):
            rows = slice(P * t, P * t + P)
            tt = ring.tile([P, ng * GRP], F32, name="tt", tag="tt", bufs=T_BUFS, align_bytes=64)
            t_tiles[(b, t)] = tt
            for l in range(ng):
                cols = slice(GRP * (g0 + l), GRP * (g0 + l) + GRP)
                pp = psum.tile([P, GRP], F32, name="pp", tag="pp", bufs=PP_BUFS)
                nc.tensor.matmul_mx(
                    out=pp,
                    lhsT=y_codes[:, rows].bitcast(FP8X4),
                    lhsT_scale=y_scales[:, rows],
                    rhs=p_codes[:, cols].bitcast(FP8X4),
                    rhs_scale=p_scales[:, cols],
                    start=True,
                    stop=True,
                )
                nc.vector.scalar_tensor_tensor(
                    out=tt[:, GRP * l : GRP * l + GRP],
                    in0=pp,
                    scalar=ee[:, t : t + 1],
                    in1=q_sb[:, cols],
                    op0=ALU.subtract,
                    op1=ALU.mult,
                )

        gate_rr = {0: rr}
        gate_ln = {}

        def gate(name, probe, value):
            z = keep.tile([P, value.shape[1]], F32, name=name)
            nc.scalar.copy(out=z[:, 0:1], in_=probe)
            nc.scalar.copy(out=z, in_=value)
            return z

        def roots(b, ng, t):
            rr = gate_rr[b]
            tt = t_tiles[(b, t)]
            yy = ring.tile([P, ng * GRP], F32, name="yy", tag="y", bufs=Y_BUFS, align_bytes=64)
            y_tiles[(b, t)] = yy
            nc.scalar.activation(out=yy, in_=tt, func=ACT.Sqrt, scale=rr[:, t : t + 1], bias=nr[:, t : t + 1])
            nc.scalar.activation(out=tt, in_=tt, func=ACT.Sqrt, scale=rr[:, t : t + 1], bias=omr[:, t : t + 1])

        def add_roots(b, t):
            yy = y_tiles[(b, t)]
            nc.vector.scalar_tensor_tensor(out=yy, in0=yy, scalar=0.0, in1=t_tiles[(b, t)], op0=ALU.max, op1=ALU.add)
            if G_CLAMP:
                nc.gpsimd.tensor_scalar(out=yy, in0=yy, scalar1=Y_MAX, scalar2=1.0, op0=ALU.min, op1=ALU.max)

        def log_(b, t, part=None):
            yy = y_tiles[(b, t)]
            if part is not None:
                yy = yy[:, part[0] : part[1]]
            nc.scalar.activation(out=yy, in_=yy, func=ACT.Ln, bias=gate_ln[b])

        def finish(b, g0, ng, t, part=None):
            yy = y_tiles[(b, t)]
            if part is not None:
                yy = yy[:, part[0] : part[1]]
                nc.vector.tensor_scalar(out=yy, in0=yy, scalar1=-K_OUT, scalar2=LOGIT_MIN, op0=ALU.mult, op1=ALU.max)
                nc.sync.dma_start(out=lg_v[:, t, GRP * g0 + part[0] : GRP * g0 + part[1]], in_=yy)
                return
            k_out = -K_OUT
            if G_CLAMP and G_FIN[t] == "G":
                nc.gpsimd.tensor_scalar(out=yy, in0=yy, scalar1=k_out, scalar2=0.0, op0=ALU.mult, op1=ALU.add)
            else:
                nc.vector.tensor_scalar(out=yy, in0=yy, scalar1=k_out, scalar2=LOGIT_MIN, op0=ALU.mult, op1=ALU.max)
            nc.sync.dma_start(out=lg_v[:, t, GRP * g0 : GRP * (g0 + ng)], in_=yy)

        w3_prep()
        h_transpose(0, H_COPY[0])
        h_transpose(1, H_COPY[1])
        h_quant(0)
        h_transpose(2, H_COPY[2])
        h_transpose(3, H_COPY[3])
        h_quant(1)
        for t in range(NT):
            u_tile(t)
        row_stats()
        for t in range(NT):
            hyp_scale(t)
            hyp_transpose(t, Y_COPY[t])
            if t % 4 == 3:
                nc.sync.dma_start(out=hy_v[:, t - 3 : t + 1, :], in_=hy[t // 4])
                hyp_quant(t // 4)
        row_stats2()
        for g in range(BLOCKS[0]):
            p_group(g, P_COPY[g][0], P_COPY[g][1], Q_COPY[g])

        g0 = 0
        for b, ng in enumerate(BLOCKS):
            for t in range(min(AHEAD, NT)):
                products(b, g0, ng, t)
            for t in range(NT):
                roots(b, ng, t)
                if t + AHEAD < NT:
                    products(b, g0, ng, t + AHEAD)
                add_roots(b, t)
            gate_ln[b] = gate("gate_ln%d" % b, t_tiles[(b, NT - 1)][:, 0:1], zero)
            for t in range(NT):
                if t == NT - 1 and b + 1 == len(BLOCKS) and LAST_SPLIT > 1:
                    w = ng * GRP // LAST_SPLIT
                    for k in range(LAST_SPLIT):
                        log_(b, t, (w * k, w * k + w))
                        finish(b, g0, ng, t, (w * k, w * k + w))
                    continue
                log_(b, t)
                if t == NT - 1 and b + 1 < len(BLOCKS):
                    gate_rr[b + 1] = gate("gate_rr%d" % (b + 1), y_tiles[(b, t)][:, 0:1], rr)
                finish(b, g0, ng, t)
            if b + 1 < len(BLOCKS):
                for g in range(g0 + ng, g0 + ng + BLOCKS[b + 1]):
                    p_group(g, P_COPY[g][0], P_COPY[g][1], Q_COPY[g])
            g0 += ng
